import numpy as np
import ml_dtypes


def mxq(x, axis, fmt="e4m3"):
    dtype, down = {"e4m3": (ml_dtypes.float8_e4m3fn, 7), "e5m2": (ml_dtypes.float8_e5m2, 14)}[fmt]
    v = np.moveaxis(np.asarray(x, np.float32).astype(ml_dtypes.bfloat16).astype(np.float64), axis, -1)
    blocks = v.reshape(v.shape[:-1] + (-1, 32))
    amax = np.abs(blocks).max(-1, keepdims=True)
    byte = np.maximum(np.where(amax > 0, np.frexp(amax)[1] - 1 + 127, 0) - down, 1)
    scale = np.exp2(byte - 127.0)
    codes = (blocks / scale).astype(np.float32).astype(dtype).astype(np.float64)
    return np.moveaxis((codes * scale).reshape(v.shape), -1, axis)


WIDE = False


def mx_kscale(k):
    if not WIDE:
        return np.ones(k)
    levels = np.array([10, -10, 5, -5, 0])
    if k % 512:
        return np.exp2(np.random.permutation(np.resize(levels, k // 32))).repeat(32)
    a = np.empty((k // 512, 16))
    for p in range(k // 512):
        a[p, :8] = np.random.permutation(np.resize(levels, 8))
        for g in range(8):
            far = levels[np.abs(levels - a[p, g]) >= 10]
            a[p, g + 8] = far[np.random.randint(len(far))]
    return np.exp2(a.ravel()).repeat(32)


BF16 = ml_dtypes.bfloat16


def bf(x):
    return np.asarray(x, np.float32).astype(BF16)


def f64(x):
    return np.asarray(x).astype(np.float64)


B, S, E, H, KVH, D = 1, 512, 2048, 16, 4, 128


def rope(t, cos, sin):
    tr = t.reshape(t.shape[:-1] + (-1, 2))
    xr, xi = tr[..., 0], tr[..., 1]
    c = cos[None, :, None, :]
    n = sin[None, :, None, :]
    return np.stack([xr * c - xi * n, xr * n + xi * c], axis=-1).reshape(t.shape)


def setup_inputs():
    s = mx_kscale(E)
    a = np.sqrt(2.0 / E)
    ang = np.outer(np.arange(S), 1.0 / (10000.0 ** (np.arange(0, D, 2) / D)))
    return {"x": bf(np.random.standard_normal((B, S, E)) * s),
            "wq_w": bf(np.random.standard_normal((H * D, E)) * a / s[None, :]),
            "wk_w": bf(np.random.standard_normal((KVH * D, E)) * a / s[None, :]),
            "wv_w": bf(np.random.standard_normal((KVH * D, E)) * a / s[None, :]),
            "freqs_cos": bf(np.cos(ang)), "freqs_sin": bf(np.sin(ang))}


def reference(x, wq_w, wk_w, wv_w, freqs_cos, freqs_sin):
    xq = mxq(f64(x), 2, "e4m3")
    q = (xq @ mxq(f64(wq_w), 1, "e4m3").T).reshape(B, S, H, D)
    k = (xq @ mxq(f64(wk_w), 1, "e4m3").T).reshape(B, S, KVH, D)
    v = (xq @ mxq(f64(wv_w), 1, "e4m3").T).reshape(B, S, KVH, D)
    c, n = f64(freqs_cos), f64(freqs_sin)
    return rope(q, c, n), rope(k, c, n), v

@@ -1,0 +1,181 @@
+from contextlib import ExitStack
+
+import concourse.mybir as mybir
+from concourse.masks import make_identity
+
+F32 = mybir.dt.float32
+BF16 = mybir.dt.bfloat16
+U32 = mybir.dt.uint32
+U8 = mybir.dt.uint8
+FP8X4 = mybir.dt.float8_e4m3fn_x4
+MULT = mybir.AluOpType.mult
+ADD = mybir.AluOpType.add
+
+P = 128
+S = 512
+K = 2048
+D = 128
+K_PASS = 4 * P
+PASSES = K // K_PASS
+WORDS_PASS = K_PASS // 2
+HALVES = 2
+ROW_TILES = 2
+BLOCK = ROW_TILES * P
+TOKEN_BLOCKS = S // BLOCK
+TOKEN_TILES = S // P
+HEADS_BLOCK = BLOCK // D
+STORE_COLS = 2 * BLOCK
+
+FLOPS = 2 * S * K * (2048 + 512 + 512)
+
+
+def tile_attention_pa_kernel(
+    tc, x, wq_w, wk_w, wv_w, freqs_cos, freqs_sin, out_0, out_1, out_2
+):
+    nc = tc.nc
+    with ExitStack() as ctx:
+        ctx.enter_context(tc.manual_schedule())
+
+        const = ctx.enter_context(tc.tile_pool(name="const", bufs=1))
+        psum_turn = ctx.enter_context(tc.psum_pool(name="psum_turn", bufs=PASSES))
+        psum_acc = ctx.enter_context(tc.psum_pool(name="psum_acc", bufs=2 * TOKEN_BLOCKS))
+
+        row_blocks = [x[0].rearrange("(p b a) k -> b p (a k)", b=TOKEN_BLOCKS, a=ROW_TILES)[b] for b in range(TOKEN_BLOCKS)]
+        weight_blocks = []
+        for weight, out, rotated in ((wq_w, out_0, True), (wk_w, out_1, True), (wv_w, out_2, False)):
+            out_view = out[0].rearrange("(p m) h d -> p m (h d)", m=TOKEN_TILES)
+            blocks_view = weight.rearrange("(b p a) k -> b p (a k)", p=P, a=ROW_TILES)
+            for b in range(weight.shape[0] // BLOCK):
+                row_blocks.append(blocks_view[b])
+                weight_blocks.append((out_view, b * BLOCK, rotated))
+        n_blocks = len(row_blocks)
+        n_weight_blocks = len(weight_blocks)
+
+        rows_pool = ctx.enter_context(tc.tile_pool(name="rows", bufs=n_blocks))
+        grouped_pool = ctx.enter_context(tc.tile_pool(name="grouped", bufs=3))
+        x_mx_pool = ctx.enter_context(tc.tile_pool(name="x_mx", bufs=TOKEN_BLOCKS))
+        w_mx_pool = ctx.enter_context(tc.tile_pool(name="w_mx", bufs=4))
+        product_pool = ctx.enter_context(tc.tile_pool(name="product", bufs=4))
+        result_pool = ctx.enter_context(tc.tile_pool(name="result", bufs=6))
+
+        rows_sb = []
+        for block_rows in row_blocks:
+            rows = rows_pool.tile([P, ROW_TILES * K], BF16)
+            nc.sync.dma_start(out=rows[:], in_=block_rows)
+            rows_sb.append(rows)
+
+        ident = const.tile([P, P], F32)
+        make_identity(nc, ident[:])
+        cos_sb = const.tile([P, TOKEN_TILES, D // 2], BF16)
+        sin_sb = const.tile([P, TOKEN_TILES, D // 2], BF16)
+        nc.scalar.dma_start(out=cos_sb[:], in_=freqs_cos.rearrange("(p m) j -> p m j", m=TOKEN_TILES))
+        nc.scalar.dma_start(out=sin_sb[:], in_=freqs_sin.rearrange("(p m) j -> p m j", m=TOKEN_TILES))
+        factors = const.tile([P, TOKEN_TILES, 2, D // 2, 2], F32)
+        nc.vector.tensor_copy(out=factors[:, :, 0, :, 0:1], in_=cos_sb[:].unsqueeze(3))
+        nc.vector.tensor_copy(out=factors[:, :, 0, :, 1:2], in_=sin_sb[:].unsqueeze(3))
+        nc.vector.tensor_scalar_mul(out=factors[:, :, 1, :, 0:1], in0=sin_sb[:].unsqueeze(3), scalar1=-1.0)
+        nc.vector.tensor_copy(out=factors[:, :, 1, :, 1:2], in_=cos_sb[:].unsqueeze(3))
+
+        def turn_block(rows):
+            words = rows[:].bitcast(F32)
+            grouped = grouped_pool.tile([P, PASSES * BLOCK * 4], BF16, align_bytes=64)
+            grouped_words = grouped[:].bitcast(F32)
+            for g in range(PASSES):
+                bank = psum_turn.tile([P, ROW_TILES, HALVES, P], F32)
+                for a in range(ROW_TILES):
+                    for u in range(HALVES):
+                        first = a * (K // 2) + g * WORDS_PASS
+                        nc.tensor.transpose(bank[:, a, u, :], words[:, first + u : first + WORDS_PASS : HALVES], ident[:])
+                nc.scalar.copy(
+                    out=grouped_words[:, g * BLOCK * HALVES : (g + 1) * BLOCK * HALVES].rearrange(
+                        "p (a r u) -> p a r u", a=ROW_TILES, u=HALVES
+                    ),
+                    in_=bank[:].rearrange("p a u r -> p a r u"),
+                )
+            return grouped
+
+        def quantise_block(pool, grouped):
+            codes = pool.tile([P, PASSES * BLOCK], U32, align_bytes=64)
+            scales = pool.tile([P, PASSES * BLOCK], U8, align_bytes=64)
+            nc.vector.quantize_mx(out=codes[:].bitcast(FP8X4), scales=scales[:], in_=grouped[:])
+            return codes, scales
+
+        def multiply_block(x_mx, w_mx):
+            w_codes, w_scales = w_mx
+            banks = []
+            for x_codes, x_scales in x_mx:
+                acc = psum_acc.tile([P, ROW_TILES * BLOCK], F32)
+                for a in range(ROW_TILES):
+                    for g in range(PASSES):
+                        tokens = slice(g * BLOCK + a * P, g * BLOCK + (a + 1) * P)
+                        features = slice(g * BLOCK, (g + 1) * BLOCK)
+                        nc.tensor.matmul_mx(
+                            out=acc[:, a * BLOCK : (a + 1) * BLOCK],
+                            lhsT=x_codes[:, tokens].bitcast(FP8X4),
+                            lhsT_scale=x_scales[:, tokens],
+                            rhs=w_codes[:, features].bitcast(FP8X4),
+                            rhs_scale=w_scales[:, features],
+                            start=(g == 0),
+                            stop=(g == PASSES - 1),
+                        )
+                banks.append(acc)
+            return banks
+
+        product_shape = [P, ROW_TILES, 2, HEADS_BLOCK, D // 2, 2]
+
+        def multiply_by_factors(acc, token_block):
+            tiles = slice(token_block * ROW_TILES, (token_block + 1) * ROW_TILES)
+            product = product_pool.tile([P, ROW_TILES, 2, BLOCK], F32)
+            nc.vector.tensor_tensor(
+                out=product[:].rearrange("p m w (h j e) -> p m w h j e", h=HEADS_BLOCK, e=2),
+                in0=acc[:]
+                .rearrange("p (m w h j) -> p m w h j", m=ROW_TILES, w=2, h=HEADS_BLOCK)
+                .unsqueeze(5)
+                .to_broadcast(product_shape),
+                in1=factors[:, tiles].unsqueeze(3).to_broadcast(product_shape),
+                op=MULT,
+            )
+            return product
+
+        results = {}
+
+        def finish_block(w, banks):
+            out_view, first_col, rotated = weight_blocks[w]
+            store_first = first_col // STORE_COLS * STORE_COLS
+            cols = slice(first_col - store_first, first_col - store_first + BLOCK)
+            if first_col == store_first:
+                for t in range(TOKEN_BLOCKS):
+                    results[t] = result_pool.tile([P, ROW_TILES, STORE_COLS], F32, name="result")
+            if rotated:
+                products = [multiply_by_factors(banks[t], t) for t in range(TOKEN_BLOCKS)]
+                for t in range(TOKEN_BLOCKS):
+                    nc.gpsimd.tensor_tensor(
+                        out=results[t][:, :, cols], in0=products[t][:, :, 0, :], in1=products[t][:, :, 1, :], op=ADD
+                    )
+            else:
+                for t in range(TOKEN_BLOCKS):
+                    nc.scalar.copy(
+                        out=results[t][:, :, cols].rearrange("p m (r e) -> p m r e", e=2),
+                        in_=banks[t][:].rearrange("p (m e r) -> p m r e", m=ROW_TILES, e=2),
+                    )
+            if first_col + BLOCK == store_first + STORE_COLS:
+                for t in range(TOKEN_BLOCKS):
+                    nc.sync.dma_start(
+                        out=out_view[:, t * ROW_TILES : (t + 1) * ROW_TILES, store_first : store_first + STORE_COLS],
+                        in_=results[t][:],
+                    )
+
+        grouped = {}
+        mx = {}
+        banks = {}
+        for step in range(n_blocks + 3):
+            if step < n_blocks:
+                grouped[step] = turn_block(rows_sb[step])
+            if 0 <= step - 1 < n_blocks:
+                pool = x_mx_pool if step - 1 < TOKEN_BLOCKS else w_mx_pool
+                mx[step - 1] = quantise_block(pool, grouped[step - 1])
+            w = step - 2 - TOKEN_BLOCKS
+            if 0 <= w < n_weight_blocks:
+                banks[w] = multiply_block([mx[t] for t in range(TOKEN_BLOCKS)], mx[w + TOKEN_BLOCKS])
+            if 0 <= w - 1 < n_weight_blocks:
+                finish_block(w - 1, banks[w - 1])

@@ -52,6 +52,7 @@ def tile_attention_pa_kernel(
         n_weight_blocks = len(weight_blocks)
 
         rows_pool = ctx.enter_context(tc.tile_pool(name="rows", bufs=n_blocks))
+        sorted_pool = ctx.enter_context(tc.tile_pool(name="sorted", bufs=2))
         grouped_pool = ctx.enter_context(tc.tile_pool(name="grouped", bufs=3))
         x_mx_pool = ctx.enter_context(tc.tile_pool(name="x_mx", bufs=TOKEN_BLOCKS))
         w_mx_pool = ctx.enter_context(tc.tile_pool(name="w_mx", bufs=4))
@@ -76,23 +77,21 @@ def tile_attention_pa_kernel(
         nc.vector.tensor_scalar_mul(out=factors[:, :, 1, :, 0:1], in0=sin_sb[:].unsqueeze(3), scalar1=-1.0)
         nc.vector.tensor_copy(out=factors[:, :, 1, :, 1:2], in_=cos_sb[:].unsqueeze(3))
 
-        def turn_block(rows):
-            words = rows[:].bitcast(F32)
-            grouped = grouped_pool.tile([P, PASSES * BLOCK * 4], BF16, align_bytes=64)
-            grouped_words = grouped[:].bitcast(F32)
-            for g in range(PASSES):
-                bank = psum_turn.tile([P, ROW_TILES, HALVES, P], F32)
-                for a in range(ROW_TILES):
-                    for u in range(HALVES):
-                        first = a * (K // 2) + g * WORDS_PASS
-                        nc.tensor.transpose(bank[:, a, u, :], words[:, first + u : first + WORDS_PASS : HALVES], ident[:])
-                nc.scalar.copy(
-                    out=grouped_words[:, g * BLOCK * HALVES : (g + 1) * BLOCK * HALVES].rearrange(
-                        "p (a r u) -> p a r u", a=ROW_TILES, u=HALVES
-                    ),
-                    in_=bank[:].rearrange("p a u r -> p a r u"),
-                )
-            return grouped
+        def sort_pass(rows, sorted_words, g, copy):
+            words = rows[:].bitcast(F32).rearrange("p (a g j u) -> p a g u j", a=ROW_TILES, g=PASSES, u=HALVES)
+            copy(out=sorted_words[:, g], in_=words[:, :, g])
+
+        def turn_pass(sorted_words, grouped, g, copy):
+            bank = psum_turn.tile([P, ROW_TILES, HALVES, P], F32)
+            for a in range(ROW_TILES):
+                for u in range(HALVES):
+                    nc.tensor.transpose(bank[:, a, u, :], sorted_words[:, g, a, u, :], ident[:])
+            copy(
+                out=grouped[:]
+                .bitcast(F32)[:, g * BLOCK * HALVES : (g + 1) * BLOCK * HALVES]
+                .rearrange("p (a r u) -> p a r u", a=ROW_TILES, u=HALVES),
+                in_=bank[:].rearrange("p a u r -> p a r u"),
+            )
 
         def quantise_block(pool, grouped):
             codes = pool.tile([P, PASSES * BLOCK], U32, align_bytes=64)
@@ -165,17 +164,30 @@ def tile_attention_pa_kernel(
                         in_=results[t][:],
                     )
 
+        n_rotated = sum(1 for block in weight_blocks if block[2])
+        sorted_words = {}
         grouped = {}
         mx = {}
         banks = {}
+        sorted_words[0] = sorted_pool.tile([P, PASSES, ROW_TILES, HALVES, P], F32, name="sorted_words")
+        for g in range(PASSES):
+            sort_pass(rows_sb[0], sorted_words[0], g, nc.vector.tensor_copy)
         for step in range(n_blocks + 3):
-            if step < n_blocks:
-                grouped[step] = turn_block(rows_sb[step])
+            w = step - 2 - TOKEN_BLOCKS
+            vector_rotates = 0 <= w - 1 < n_rotated
+            if 0 <= w - 1 < n_weight_blocks:
+                finish_block(w - 1, banks[w - 1])
             if 0 <= step - 1 < n_blocks:
                 pool = x_mx_pool if step - 1 < TOKEN_BLOCKS else w_mx_pool
                 mx[step - 1] = quantise_block(pool, grouped[step - 1])
-            w = step - 2 - TOKEN_BLOCKS
+            if step < n_blocks:
+                grouped[step] = grouped_pool.tile([P, PASSES * BLOCK * 4], BF16, align_bytes=64, name="grouped")
+                if step + 1 < n_blocks:
+                    sorted_words[step + 1] = sorted_pool.tile([P, PASSES, ROW_TILES, HALVES, P], F32, name="sorted_words")
+                for g in range(PASSES):
+                    by_vector = vector_rotates and g == PASSES - 1
+                    turn_pass(sorted_words[step], grouped[step], g, nc.vector.tensor_copy if by_vector else nc.scalar.copy)
+                    if step + 1 < n_blocks:
+                        sort_pass(rows_sb[step + 1], sorted_words[step + 1], g, nc.scalar.copy if vector_rotates else nc.vector.tensor_copy)
             if 0 <= w < n_weight_blocks:
                 banks[w] = multiply_block([mx[t] for t in range(TOKEN_BLOCKS)], mx[w + TOKEN_BLOCKS])
-            if 0 <= w - 1 < n_weight_blocks:
-                finish_block(w - 1, banks[w - 1])

@@ -59,33 +59,40 @@ def tile_attention_pa_kernel(
         product_pool = ctx.enter_context(tc.tile_pool(name="product", bufs=4))
         result_pool = ctx.enter_context(tc.tile_pool(name="result", bufs=6))
 
+        cos_sb = const.tile([P, TOKEN_TILES, D // 2], BF16)
+        sin_sb = const.tile([P, TOKEN_TILES, D // 2], BF16)
         rows_sb = []
         for block_rows in row_blocks:
             rows = rows_pool.tile([P, ROW_TILES * K], BF16)
             nc.sync.dma_start(out=rows[:], in_=block_rows)
             rows_sb.append(rows)
+            if len(rows_sb) == TOKEN_BLOCKS + 2:
+                nc.sync.dma_start(out=cos_sb[:], in_=freqs_cos.rearrange("(p m) j -> p m j", m=TOKEN_TILES))
+                nc.sync.dma_start(out=sin_sb[:], in_=freqs_sin.rearrange("(p m) j -> p m j", m=TOKEN_TILES))
 
         ident = const.tile([P, P], F32)
         make_identity(nc, ident[:])
-        cos_sb = const.tile([P, TOKEN_TILES, D // 2], BF16)
-        sin_sb = const.tile([P, TOKEN_TILES, D // 2], BF16)
-        nc.scalar.dma_start(out=cos_sb[:], in_=freqs_cos.rearrange("(p m) j -> p m j", m=TOKEN_TILES))
-        nc.scalar.dma_start(out=sin_sb[:], in_=freqs_sin.rearrange("(p m) j -> p m j", m=TOKEN_TILES))
         factors = const.tile([P, TOKEN_TILES, 2, D // 2, 2], F32)
-        nc.vector.tensor_copy(out=factors[:, :, 0, :, 0:1], in_=cos_sb[:].unsqueeze(3))
-        nc.vector.tensor_copy(out=factors[:, :, 0, :, 1:2], in_=sin_sb[:].unsqueeze(3))
-        nc.vector.tensor_scalar_mul(out=factors[:, :, 1, :, 0:1], in0=sin_sb[:].unsqueeze(3), scalar1=-1.0)
-        nc.vector.tensor_copy(out=factors[:, :, 1, :, 1:2], in_=cos_sb[:].unsqueeze(3))
+        nc.gpsimd.tensor_copy(out=factors[:, :, 0, :, 0:1], in_=cos_sb[:].unsqueeze(3))
+        nc.gpsimd.tensor_copy(out=factors[:, :, 0, :, 1:2], in_=sin_sb[:].unsqueeze(3))
+        nc.gpsimd.tensor_scalar_mul(out=factors[:, :, 1, :, 0:1], in0=sin_sb[:].unsqueeze(3), scalar1=-1.0)
+        nc.gpsimd.tensor_copy(out=factors[:, :, 1, :, 1:2], in_=cos_sb[:].unsqueeze(3))
 
         def sort_pass(rows, sorted_words, g, copy):
             words = rows[:].bitcast(F32).rearrange("p (a g j u) -> p a g u j", a=ROW_TILES, g=PASSES, u=HALVES)
             copy(out=sorted_words[:, g], in_=words[:, :, g])
 
-        def turn_pass(sorted_words, grouped, g, copy):
+        def turn_pass(rows, sorted_words, grouped, g, copy):
             bank = psum_turn.tile([P, ROW_TILES, HALVES, P], F32)
+            words = rows[:].bitcast(F32)
             for a in range(ROW_TILES):
                 for u in range(HALVES):
-                    nc.tensor.transpose(bank[:, a, u, :], sorted_words[:, g, a, u, :], ident[:])
+                    if sorted_words is None:
+                        first = a * (K // 2) + g * WORDS_PASS
+                        half = words[:, first + u : first + WORDS_PASS : HALVES]
+                    else:
+                        half = sorted_words[:, g, a, u, :]
+                    nc.tensor.transpose(bank[:, a, u, :], half, ident[:])
             copy(
                 out=grouped[:]
                 .bitcast(F32)[:, g * BLOCK * HALVES : (g + 1) * BLOCK * HALVES]
@@ -182,12 +189,12 @@ def tile_attention_pa_kernel(
                 mx[step - 1] = quantise_block(pool, grouped[step - 1])
             if step < n_blocks:
                 grouped[step] = grouped_pool.tile([P, PASSES * BLOCK * 4], BF16, align_bytes=64, name="grouped")
-                if step + 1 < n_blocks:
+                sort_next = step + 1 < n_blocks and not vector_rotates
+                if sort_next:
                     sorted_words[step + 1] = sorted_pool.tile([P, PASSES, ROW_TILES, HALVES, P], F32, name="sorted_words")
                 for g in range(PASSES):
-                    by_vector = vector_rotates and g == PASSES - 1
-                    turn_pass(sorted_words[step], grouped[step], g, nc.vector.tensor_copy if by_vector else nc.scalar.copy)
-                    if step + 1 < n_blocks:
-                        sort_pass(rows_sb[step + 1], sorted_words[step + 1], g, nc.scalar.copy if vector_rotates else nc.vector.tensor_copy)
+                    turn_pass(rows_sb[step], sorted_words.get(step), grouped[step], g, nc.scalar.copy)
+                    if sort_next:
+                        sort_pass(rows_sb[step + 1], sorted_words[step + 1], g, nc.vector.tensor_copy)
             if 0 <= w < n_weight_blocks:
                 banks[w] = multiply_block([mx[t] for t in range(TOKEN_BLOCKS)], mx[w + TOKEN_BLOCKS])

@@ -21,10 +21,16 @@ WORDS_PASS = K_PASS // 2
 HALVES = 2
 ROW_TILES = 2
 BLOCK = ROW_TILES * P
+PAIR = 2
+UNITS = ROW_TILES * PASSES // PAIR
 TOKEN_BLOCKS = S // BLOCK
 TOKEN_TILES = S // P
 HEADS_BLOCK = BLOCK // D
 STORE_COLS = 2 * BLOCK
+SPLIT_LOADS = 5
+FIRST_SORTED = 5
+SCALAR_SORTS = 3
+VECTOR_SORTS = 0
 
 FLOPS = 2 * S * K * (2048 + 512 + 512)
 
@@ -37,14 +43,14 @@ def tile_attention_pa_kernel(
         ctx.enter_context(tc.manual_schedule())
 
         const = ctx.enter_context(tc.tile_pool(name="const", bufs=1))
-        psum_turn = ctx.enter_context(tc.psum_pool(name="psum_turn", bufs=PASSES))
+        psum_turn = ctx.enter_context(tc.psum_pool(name="psum_turn", bufs=UNITS))
         psum_acc = ctx.enter_context(tc.psum_pool(name="psum_acc", bufs=2 * TOKEN_BLOCKS))
 
-        row_blocks = [x[0].rearrange("(p b a) k -> b p (a k)", b=TOKEN_BLOCKS, a=ROW_TILES)[b] for b in range(TOKEN_BLOCKS)]
+        row_blocks = [x[0].rearrange("(p b a) k -> b a p k", b=TOKEN_BLOCKS, a=ROW_TILES)[b] for b in range(TOKEN_BLOCKS)]
         weight_blocks = []
         for weight, out, rotated in ((wq_w, out_0, True), (wk_w, out_1, True), (wv_w, out_2, False)):
             out_view = out[0].rearrange("(p m) h d -> p m (h d)", m=TOKEN_TILES)
-            blocks_view = weight.rearrange("(b p a) k -> b p (a k)", p=P, a=ROW_TILES)
+            blocks_view = weight.rearrange("(b p a) k -> b a p k", p=P, a=ROW_TILES)
             for b in range(weight.shape[0] // BLOCK):
                 row_blocks.append(blocks_view[b])
                 weight_blocks.append((out_view, b * BLOCK, rotated))
@@ -63,8 +69,12 @@ def tile_attention_pa_kernel(
         sin_sb = const.tile([P, TOKEN_TILES, D // 2], BF16)
         rows_sb = []
         for block_rows in row_blocks:
-            rows = rows_pool.tile([P, ROW_TILES * K], BF16)
-            nc.sync.dma_start(out=rows[:], in_=block_rows)
+            rows = rows_pool.tile([P, ROW_TILES, K], BF16)
+            if len(rows_sb) < SPLIT_LOADS:
+                for a in range(ROW_TILES):
+                    nc.sync.dma_start(out=rows[:, a, :], in_=block_rows[a])
+            else:
+                nc.sync.dma_start(out=rows[:], in_=block_rows.rearrange("a p k -> p a k"))
             rows_sb.append(rows)
             if len(rows_sb) == TOKEN_BLOCKS + 2:
                 nc.sync.dma_start(out=cos_sb[:], in_=freqs_cos.rearrange("(p m) j -> p m j", m=TOKEN_TILES))
@@ -78,26 +88,30 @@ def tile_attention_pa_kernel(
         nc.gpsimd.tensor_scalar_mul(out=factors[:, :, 1, :, 0:1], in0=sin_sb[:].unsqueeze(3), scalar1=-1.0)
         nc.gpsimd.tensor_copy(out=factors[:, :, 1, :, 1:2], in_=cos_sb[:].unsqueeze(3))
 
-        def sort_pass(rows, sorted_words, g, copy):
-            words = rows[:].bitcast(F32).rearrange("p (a g j u) -> p a g u j", a=ROW_TILES, g=PASSES, u=HALVES)
-            copy(out=sorted_words[:, g], in_=words[:, :, g])
+        def sort_unit(rows, sorted_words, q, copy):
+            words = rows[:].rearrange("p a k -> p (a k)").bitcast(F32)
+            copy(
+                out=sorted_words[:, q],
+                in_=words.rearrange("p (q g j u) -> p q g u j", q=UNITS, g=PAIR, u=HALVES)[:, q],
+            )
 
-        def turn_pass(rows, sorted_words, grouped, g, copy):
-            bank = psum_turn.tile([P, ROW_TILES, HALVES, P], F32)
-            words = rows[:].bitcast(F32)
-            for a in range(ROW_TILES):
+        def turn_unit(rows, sorted_words, grouped, q, copy):
+            a, pair = divmod(q, PASSES // PAIR)
+            words = rows[:, a, :].bitcast(F32)
+            bank = psum_turn.tile([P, PAIR, HALVES, P], F32)
+            for g in range(PAIR):
                 for u in range(HALVES):
                     if sorted_words is None:
-                        first = a * (K // 2) + g * WORDS_PASS
+                        first = (pair * PAIR + g) * WORDS_PASS
                         half = words[:, first + u : first + WORDS_PASS : HALVES]
                     else:
-                        half = sorted_words[:, g, a, u, :]
-                    nc.tensor.transpose(bank[:, a, u, :], half, ident[:])
+                        half = sorted_words[:, q, g, u, :]
+                    nc.tensor.transpose(bank[:, g, u, :], half, ident[:])
             copy(
                 out=grouped[:]
-                .bitcast(F32)[:, g * BLOCK * HALVES : (g + 1) * BLOCK * HALVES]
-                .rearrange("p (a r u) -> p a r u", a=ROW_TILES, u=HALVES),
-                in_=bank[:].rearrange("p a u r -> p a r u"),
+                .bitcast(F32)
+                .rearrange("p (g a r u) -> p g a r u", g=PASSES, a=ROW_TILES, u=HALVES)[:, pair * PAIR : (pair + 1) * PAIR, a],
+                in_=bank[:].rearrange("p g u r -> p g r u"),
             )
 
         def quantise_block(pool, grouped):
@@ -106,24 +120,28 @@ def tile_attention_pa_kernel(
             nc.vector.quantize_mx(out=codes[:].bitcast(FP8X4), scales=scales[:], in_=grouped[:])
             return codes, scales
 
-        def multiply_block(x_mx, w_mx):
+        def multiply_tile(acc, x_mx, a, w_mx):
+            x_codes, x_scales = x_mx
             w_codes, w_scales = w_mx
+            for g in range(PASSES):
+                tokens = slice(g * BLOCK + a * P, g * BLOCK + (a + 1) * P)
+                features = slice(g * BLOCK, (g + 1) * BLOCK)
+                nc.tensor.matmul_mx(
+                    out=acc,
+                    lhsT=x_codes[:, tokens].bitcast(FP8X4),
+                    lhsT_scale=x_scales[:, tokens],
+                    rhs=w_codes[:, features].bitcast(FP8X4),
+                    rhs_scale=w_scales[:, features],
+                    start=(g == 0),
+                    stop=(g == PASSES - 1),
+                )
+
+        def multiply_block(x_mx, w_mx):
             banks = []
-            for x_codes, x_scales in x_mx:
-                acc = psum_acc.tile([P, ROW_TILES * BLOCK], F32)
+            for t in range(TOKEN_BLOCKS):
+                acc = psum_acc.tile([P, ROW_TILES * BLOCK], F32, name="acc")
                 for a in range(ROW_TILES):
-                    for g in range(PASSES):
-                        tokens = slice(g * BLOCK + a * P, g * BLOCK + (a + 1) * P)
-                        features = slice(g * BLOCK, (g + 1) * BLOCK)
-                        nc.tensor.matmul_mx(
-                            out=acc[:, a * BLOCK : (a + 1) * BLOCK],
-                            lhsT=x_codes[:, tokens].bitcast(FP8X4),
-                            lhsT_scale=x_scales[:, tokens],
-                            rhs=w_codes[:, features].bitcast(FP8X4),
-                            rhs_scale=w_scales[:, features],
-                            start=(g == 0),
-                            stop=(g == PASSES - 1),
-                        )
+                    multiply_tile(acc[:, a * BLOCK : (a + 1) * BLOCK], x_mx[t], a, w_mx)
                 banks.append(acc)
             return banks
 
@@ -171,17 +189,12 @@ def tile_attention_pa_kernel(
                         in_=results[t][:],
                     )
 
-        n_rotated = sum(1 for block in weight_blocks if block[2])
         sorted_words = {}
         grouped = {}
         mx = {}
         banks = {}
-        sorted_words[0] = sorted_pool.tile([P, PASSES, ROW_TILES, HALVES, P], F32, name="sorted_words")
-        for g in range(PASSES):
-            sort_pass(rows_sb[0], sorted_words[0], g, nc.vector.tensor_copy)
         for step in range(n_blocks + 3):
             w = step - 2 - TOKEN_BLOCKS
-            vector_rotates = 0 <= w - 1 < n_rotated
             if 0 <= w - 1 < n_weight_blocks:
                 finish_block(w - 1, banks[w - 1])
             if 0 <= step - 1 < n_blocks:
@@ -189,12 +202,15 @@ def tile_attention_pa_kernel(
                 mx[step - 1] = quantise_block(pool, grouped[step - 1])
             if step < n_blocks:
                 grouped[step] = grouped_pool.tile([P, PASSES * BLOCK * 4], BF16, align_bytes=64, name="grouped")
-                sort_next = step + 1 < n_blocks and not vector_rotates
+                sort_next = FIRST_SORTED <= step + 1 < n_blocks
                 if sort_next:
-                    sorted_words[step + 1] = sorted_pool.tile([P, PASSES, ROW_TILES, HALVES, P], F32, name="sorted_words")
-                for g in range(PASSES):
-                    turn_pass(rows_sb[step], sorted_words.get(step), grouped[step], g, nc.scalar.copy)
-                    if sort_next:
-                        sort_pass(rows_sb[step + 1], sorted_words[step + 1], g, nc.vector.tensor_copy)
+                    sorted_words[step + 1] = sorted_pool.tile([P, SCALAR_SORTS + VECTOR_SORTS, PAIR, HALVES, P], F32, name="sorted_words")
+                for q in range(UNITS):
+                    is_sorted = step >= FIRST_SORTED and q < SCALAR_SORTS + VECTOR_SORTS
+                    turn_unit(rows_sb[step], sorted_words[step] if is_sorted else None, grouped[step], q, nc.scalar.copy)
+                    if sort_next and q < SCALAR_SORTS:
+                        sort_unit(rows_sb[step + 1], sorted_words[step + 1], q, nc.scalar.copy)
+                    elif sort_next and q < SCALAR_SORTS + VECTOR_SORTS:
+                        sort_unit(rows_sb[step + 1], sorted_words[step + 1], q, nc.vector.tensor_copy)
             if 0 <= w < n_weight_blocks:
                 banks[w] = multiply_block([mx[t] for t in range(TOKEN_BLOCKS)], mx[w + TOKEN_BLOCKS])

@@ -29,8 +29,8 @@ HEADS_BLOCK = BLOCK // D
 STORE_COLS = 2 * BLOCK
 SPLIT_LOADS = 5
 FIRST_SORTED = 5
-SCALAR_SORTS = 3
-VECTOR_SORTS = 0
+SCALAR_SORTS = 2
+VECTOR_SORTS = 1
 
 FLOPS = 2 * S * K * (2048 + 512 + 512)
 
@@ -64,6 +64,7 @@ def tile_attention_pa_kernel(
         w_mx_pool = ctx.enter_context(tc.tile_pool(name="w_mx", bufs=4))
         product_pool = ctx.enter_context(tc.tile_pool(name="product", bufs=4))
         result_pool = ctx.enter_context(tc.tile_pool(name="result", bufs=6))
+        last_pool = ctx.enter_context(tc.tile_pool(name="last", bufs=TOKEN_TILES))
 
         cos_sb = const.tile([P, TOKEN_TILES, D // 2], BF16)
         sin_sb = const.tile([P, TOKEN_TILES, D // 2], BF16)
@@ -165,11 +166,12 @@ def tile_attention_pa_kernel(
 
         def finish_block(w, banks):
             out_view, first_col, rotated = weight_blocks[w]
-            store_first = first_col // STORE_COLS * STORE_COLS
+            store_cols = STORE_COLS if rotated else BLOCK
+            store_first = first_col // store_cols * store_cols
             cols = slice(first_col - store_first, first_col - store_first + BLOCK)
             if first_col == store_first:
                 for t in range(TOKEN_BLOCKS):
-                    results[t] = result_pool.tile([P, ROW_TILES, STORE_COLS], F32, name="result")
+                    results[t] = result_pool.tile([P, ROW_TILES, store_cols], F32, name="result")
             if rotated:
                 products = [multiply_by_factors(banks[t], t) for t in range(TOKEN_BLOCKS)]
                 for t in range(TOKEN_BLOCKS):
@@ -182,20 +184,32 @@ def tile_attention_pa_kernel(
                         out=results[t][:, :, cols].rearrange("p m (r e) -> p m r e", e=2),
                         in_=banks[t][:].rearrange("p (m e r) -> p m r e", m=ROW_TILES, e=2),
                     )
-            if first_col + BLOCK == store_first + STORE_COLS:
+            if first_col + BLOCK == store_first + store_cols:
                 for t in range(TOKEN_BLOCKS):
                     nc.sync.dma_start(
-                        out=out_view[:, t * ROW_TILES : (t + 1) * ROW_TILES, store_first : store_first + STORE_COLS],
+                        out=out_view[:, t * ROW_TILES : (t + 1) * ROW_TILES, store_first : store_first + store_cols],
                         in_=results[t][:],
                     )
+
+        def multiply_and_finish_last_block(x_mx, w_mx):
+            out_view, first_col, rotated = weight_blocks[n_weight_blocks - 1]
+            assert not rotated
+            for m in range(TOKEN_TILES):
+                t, a = divmod(m, ROW_TILES)
+                acc = psum_acc.tile([P, BLOCK], F32, name="acc")
+                multiply_tile(acc[:], x_mx[t], a, w_mx)
+                last = last_pool.tile([P, BLOCK], F32)
+                copy = nc.vector.tensor_copy if m % 2 else nc.scalar.copy
+                copy(out=last[:].rearrange("p (r e) -> p r e", e=2), in_=acc[:].rearrange("p (e r) -> p r e", e=2))
+                nc.sync.dma_start(out=out_view[:, m, first_col : first_col + BLOCK], in_=last[:])
 
         sorted_words = {}
         grouped = {}
         mx = {}
         banks = {}
-        for step in range(n_blocks + 3):
+        for step in range(n_blocks + 2):
             w = step - 2 - TOKEN_BLOCKS
-            if 0 <= w - 1 < n_weight_blocks:
+            if 0 <= w - 1 < n_weight_blocks - 1:
                 finish_block(w - 1, banks[w - 1])
             if 0 <= step - 1 < n_blocks:
                 pool = x_mx_pool if step - 1 < TOKEN_BLOCKS else w_mx_pool
@@ -212,5 +226,7 @@ def tile_attention_pa_kernel(
                         sort_unit(rows_sb[step + 1], sorted_words[step + 1], q, nc.scalar.copy)
                     elif sort_next and q < SCALAR_SORTS + VECTOR_SORTS:
                         sort_unit(rows_sb[step + 1], sorted_words[step + 1], q, nc.vector.tensor_copy)
-            if 0 <= w < n_weight_blocks:
+            if 0 <= w < n_weight_blocks - 1:
                 banks[w] = multiply_block([mx[t] for t in range(TOKEN_BLOCKS)], mx[w + TOKEN_BLOCKS])
+            elif w == n_weight_blocks - 1:
+                multiply_and_finish_last_block([mx[t] for t in range(TOKEN_BLOCKS)], mx[w + TOKEN_BLOCKS])

@@ -29,8 +29,8 @@ HEADS_BLOCK = BLOCK // D
 STORE_COLS = 2 * BLOCK
 SPLIT_LOADS = 5
 FIRST_SORTED = 5
-SCALAR_SORTS = 2
-VECTOR_SORTS = 1
+SCALAR_SORTS = 3
+VECTOR_SORTS = 0
 
 FLOPS = 2 * S * K * (2048 + 512 + 512)
 
@@ -146,23 +146,21 @@ def tile_attention_pa_kernel(
                 banks.append(acc)
             return banks
 
-        product_shape = [P, ROW_TILES, 2, HEADS_BLOCK, D // 2, 2]
-
-        def multiply_by_factors(acc, token_block):
-            tiles = slice(token_block * ROW_TILES, (token_block + 1) * ROW_TILES)
-            product = product_pool.tile([P, ROW_TILES, 2, BLOCK], F32)
+        def multiply_by_factors(product, acc, token_block, first, count):
+            shape = [P, count, 2, HEADS_BLOCK, D // 2, 2]
+            tiles = slice(token_block * ROW_TILES + first, token_block * ROW_TILES + first + count)
             nc.vector.tensor_tensor(
-                out=product[:].rearrange("p m w (h j e) -> p m w h j e", h=HEADS_BLOCK, e=2),
-                in0=acc[:]
-                .rearrange("p (m w h j) -> p m w h j", m=ROW_TILES, w=2, h=HEADS_BLOCK)
+                out=product[:, first : first + count].rearrange("p m w (h j e) -> p m w h j e", h=HEADS_BLOCK, e=2),
+                in0=acc[:, first * BLOCK : (first + count) * BLOCK]
+                .rearrange("p (m w h j) -> p m w h j", m=count, w=2, h=HEADS_BLOCK)
                 .unsqueeze(5)
-                .to_broadcast(product_shape),
-                in1=factors[:, tiles].unsqueeze(3).to_broadcast(product_shape),
+                .to_broadcast(shape),
+                in1=factors[:, tiles].unsqueeze(3).to_broadcast(shape),
                 op=MULT,
             )
-            return product
 
         results = {}
+        late_adds = []
 
         def finish_block(w, banks):
             out_view, first_col, rotated = weight_blocks[w]
@@ -173,17 +171,32 @@ def tile_attention_pa_kernel(
                 for t in range(TOKEN_BLOCKS):
                     results[t] = result_pool.tile([P, ROW_TILES, store_cols], F32, name="result")
             if rotated:
-                products = [multiply_by_factors(banks[t], t) for t in range(TOKEN_BLOCKS)]
+                late_adds.clear()
                 for t in range(TOKEN_BLOCKS):
-                    nc.gpsimd.tensor_tensor(
-                        out=results[t][:, :, cols], in0=products[t][:, :, 0, :], in1=products[t][:, :, 1, :], op=ADD
-                    )
+                    product = product_pool.tile([P, ROW_TILES, 2, BLOCK], F32, name="product")
+                    if t == 0:
+                        for a in range(ROW_TILES):
+                            multiply_by_factors(product, banks[t], t, a, 1)
+                            nc.gpsimd.tensor_tensor(
+                                out=results[t][:, a, cols], in0=product[:, a, 0, :], in1=product[:, a, 1, :], op=ADD
+                            )
+                    else:
+                        multiply_by_factors(product, banks[t], t, 0, ROW_TILES)
+                        late_adds.append((results[t][:, :, cols], product[:, :, 0, :], product[:, :, 1, :]))
             else:
                 for t in range(TOKEN_BLOCKS):
                     nc.scalar.copy(
                         out=results[t][:, :, cols].rearrange("p m (r e) -> p m r e", e=2),
                         in_=banks[t][:].rearrange("p (m e r) -> p m r e", m=ROW_TILES, e=2),
                     )
+
+        def store_block(w):
+            out_view, first_col, rotated = weight_blocks[w]
+            store_cols = STORE_COLS if rotated else BLOCK
+            store_first = first_col // store_cols * store_cols
+            for out, in0, in1 in late_adds:
+                nc.vector.tensor_tensor(out=out, in0=in0, in1=in1, op=ADD)
+            late_adds.clear()
             if first_col + BLOCK == store_first + store_cols:
                 for t in range(TOKEN_BLOCKS):
                     nc.sync.dma_start(
@@ -214,6 +227,8 @@ def tile_attention_pa_kernel(
             if 0 <= step - 1 < n_blocks:
                 pool = x_mx_pool if step - 1 < TOKEN_BLOCKS else w_mx_pool
                 mx[step - 1] = quantise_block(pool, grouped[step - 1])
+            if 0 <= w - 1 < n_weight_blocks - 1:
+                store_block(w - 1)
             if step < n_blocks:
                 grouped[step] = grouped_pool.tile([P, PASSES * BLOCK * 4], BF16, align_bytes=64, name="grouped")
                 sort_next = FIRST_SORTED <= step + 1 < n_blocks

@@ -27,6 +27,7 @@ TOKEN_BLOCKS = S // BLOCK
 TOKEN_TILES = S // P
 HEADS_BLOCK = BLOCK // D
 STORE_COLS = 2 * BLOCK
+PAIRED_STORES = 2048 // BLOCK
 SPLIT_LOADS = 5
 FIRST_SORTED = 5
 SCALAR_SORTS = 3
@@ -99,7 +100,7 @@ def tile_attention_pa_kernel(
         def turn_unit(rows, sorted_words, grouped, q, copy):
             a, pair = divmod(q, PASSES // PAIR)
             words = rows[:, a, :].bitcast(F32)
-            bank = psum_turn.tile([P, PAIR, HALVES, P], F32)
+            bank = psum_turn.tile([P, PAIR, HALVES, P], F32, name="bank")
             for g in range(PAIR):
                 for u in range(HALVES):
                     if sorted_words is None:
@@ -164,7 +165,7 @@ def tile_attention_pa_kernel(
 
         def finish_block(w, banks):
             out_view, first_col, rotated = weight_blocks[w]
-            store_cols = STORE_COLS if rotated else BLOCK
+            store_cols = STORE_COLS if w < PAIRED_STORES else BLOCK
             store_first = first_col // store_cols * store_cols
             cols = slice(first_col - store_first, first_col - store_first + BLOCK)
             if first_col == store_first:
@@ -192,7 +193,7 @@ def tile_attention_pa_kernel(
 
         def store_block(w):
             out_view, first_col, rotated = weight_blocks[w]
-            store_cols = STORE_COLS if rotated else BLOCK
+            store_cols = STORE_COLS if w < PAIRED_STORES else BLOCK
             store_first = first_col // store_cols * store_cols
             for out, in0, in1 in late_adds:
                 nc.vector.tensor_tensor(out=out, in0=in0, in1=in1, op=ADD)
@@ -209,7 +210,7 @@ def tile_attention_pa_kernel(
             assert not rotated
             for m in range(TOKEN_TILES):
                 t, a = divmod(m, ROW_TILES)
-                acc = psum_acc.tile([P, BLOCK], F32, name="acc")
+                acc = psum_turn.tile([P, BLOCK], F32, name="bank")
                 multiply_tile(acc[:], x_mx[t], a, w_mx)
                 last = last_pool.tile([P, BLOCK], F32)
                 copy = nc.vector.tensor_copy if m % 2 else nc.scalar.copy
@@ -222,9 +223,12 @@ def tile_attention_pa_kernel(
         banks = {}
         for step in range(n_blocks + 2):
             w = step - 2 - TOKEN_BLOCKS
+            quantise_first = step - 1 == n_blocks - 1
+            if quantise_first:
+                mx[step - 1] = quantise_block(w_mx_pool, grouped[step - 1])
             if 0 <= w - 1 < n_weight_blocks - 1:
                 finish_block(w - 1, banks[w - 1])
-            if 0 <= step - 1 < n_blocks:
+            if 0 <= step - 1 < n_blocks and not quantise_first:
                 pool = x_mx_pool if step - 1 < TOKEN_BLOCKS else w_mx_pool
                 mx[step - 1] = quantise_block(pool, grouped[step - 1])
             if 0 <= w - 1 < n_weight_blocks - 1:
@@ -237,10 +241,9 @@ def tile_attention_pa_kernel(
                 for q in range(UNITS):
                     is_sorted = step >= FIRST_SORTED and q < SCALAR_SORTS + VECTOR_SORTS
                     turn_unit(rows_sb[step], sorted_words[step] if is_sorted else None, grouped[step], q, nc.scalar.copy)
-                    if sort_next and q < SCALAR_SORTS:
-                        sort_unit(rows_sb[step + 1], sorted_words[step + 1], q, nc.scalar.copy)
-                    elif sort_next and q < SCALAR_SORTS + VECTOR_SORTS:
-                        sort_unit(rows_sb[step + 1], sorted_words[step + 1], q, nc.vector.tensor_copy)
+                if sort_next:
+                    for q in range(SCALAR_SORTS + VECTOR_SORTS):
+                        sort_unit(rows_sb[step + 1], sorted_words[step + 1], q, nc.scalar.copy if q < SCALAR_SORTS else nc.vector.tensor_copy)
             if 0 <= w < n_weight_blocks - 1:
                 banks[w] = multiply_block([mx[t] for t in range(TOKEN_BLOCKS)], mx[w + TOKEN_BLOCKS])
             elif w == n_weight_blocks - 1:

@@ -30,8 +30,8 @@ STORE_COLS = 2 * BLOCK
 PAIRED_STORES = 2048 // BLOCK
 SPLIT_LOADS = 5
 FIRST_SORTED = 5
-SCALAR_SORTS = 3
-VECTOR_SORTS = 0
+SORTED_UNITS = 3
+SORT_AHEAD = 2
 
 FLOPS = 2 * S * K * (2048 + 512 + 512)
 
@@ -59,7 +59,7 @@ def tile_attention_pa_kernel(
         n_weight_blocks = len(weight_blocks)
 
         rows_pool = ctx.enter_context(tc.tile_pool(name="rows", bufs=n_blocks))
-        sorted_pool = ctx.enter_context(tc.tile_pool(name="sorted", bufs=2))
+        sorted_pool = ctx.enter_context(tc.tile_pool(name="sorted", bufs=SORT_AHEAD + 1))
         grouped_pool = ctx.enter_context(tc.tile_pool(name="grouped", bufs=3))
         x_mx_pool = ctx.enter_context(tc.tile_pool(name="x_mx", bufs=TOKEN_BLOCKS))
         w_mx_pool = ctx.enter_context(tc.tile_pool(name="w_mx", bufs=4))
@@ -90,12 +90,14 @@ def tile_attention_pa_kernel(
         nc.gpsimd.tensor_scalar_mul(out=factors[:, :, 1, :, 0:1], in0=sin_sb[:].unsqueeze(3), scalar1=-1.0)
         nc.gpsimd.tensor_copy(out=factors[:, :, 1, :, 1:2], in_=cos_sb[:].unsqueeze(3))
 
-        def sort_unit(rows, sorted_words, q, copy):
+        def sort_block(rows, copy):
+            sorted_words = sorted_pool.tile([P, SORTED_UNITS, PAIR, HALVES, P], F32, name="sorted_words")
             words = rows[:].rearrange("p a k -> p (a k)").bitcast(F32)
             copy(
-                out=sorted_words[:, q],
-                in_=words.rearrange("p (q g j u) -> p q g u j", q=UNITS, g=PAIR, u=HALVES)[:, q],
+                out=sorted_words[:].rearrange("p q g u j -> p (q g) u j"),
+                in_=words[:, : SORTED_UNITS * PAIR * WORDS_PASS].rearrange("p (n j u) -> p n u j", n=SORTED_UNITS * PAIR, u=HALVES),
             )
+            return sorted_words
 
         def turn_unit(rows, sorted_words, grouped, q, copy):
             a, pair = divmod(q, PASSES // PAIR)
@@ -162,6 +164,7 @@ def tile_attention_pa_kernel(
 
         results = {}
         late_adds = []
+        held_stores = []
 
         def finish_block(w, banks):
             out_view, first_col, rotated = weight_blocks[w]
@@ -199,11 +202,16 @@ def tile_attention_pa_kernel(
                 nc.vector.tensor_tensor(out=out, in0=in0, in1=in1, op=ADD)
             late_adds.clear()
             if first_col + BLOCK == store_first + store_cols:
-                for t in range(TOKEN_BLOCKS):
-                    nc.sync.dma_start(
-                        out=out_view[:, t * ROW_TILES : (t + 1) * ROW_TILES, store_first : store_first + store_cols],
-                        in_=results[t][:],
-                    )
+                stores = [
+                    (out_view[:, t * ROW_TILES : (t + 1) * ROW_TILES, store_first : store_first + store_cols], results[t])
+                    for t in range(TOKEN_BLOCKS)
+                ]
+                if rotated and not weight_blocks[w + 1][2]:
+                    held_stores.extend(stores)
+                    return
+                for out, result in stores + held_stores:
+                    nc.sync.dma_start(out=out, in_=result[:])
+                held_stores.clear()
 
         def multiply_and_finish_last_block(x_mx, w_mx):
             out_view, first_col, rotated = weight_blocks[n_weight_blocks - 1]
@@ -213,8 +221,7 @@ def tile_attention_pa_kernel(
                 acc = psum_turn.tile([P, BLOCK], F32, name="bank")
                 multiply_tile(acc[:], x_mx[t], a, w_mx)
                 last = last_pool.tile([P, BLOCK], F32)
-                copy = nc.vector.tensor_copy if m % 2 else nc.scalar.copy
-                copy(out=last[:].rearrange("p (r e) -> p r e", e=2), in_=acc[:].rearrange("p (e r) -> p r e", e=2))
+                nc.scalar.copy(out=last[:].rearrange("p (r e) -> p r e", e=2), in_=acc[:].rearrange("p (e r) -> p r e", e=2))
                 nc.sync.dma_start(out=out_view[:, m, first_col : first_col + BLOCK], in_=last[:])
 
         sorted_words = {}
@@ -235,15 +242,13 @@ def tile_attention_pa_kernel(
                 store_block(w - 1)
             if step < n_blocks:
                 grouped[step] = grouped_pool.tile([P, PASSES * BLOCK * 4], BF16, align_bytes=64, name="grouped")
-                sort_next = FIRST_SORTED <= step + 1 < n_blocks
-                if sort_next:
-                    sorted_words[step + 1] = sorted_pool.tile([P, SCALAR_SORTS + VECTOR_SORTS, PAIR, HALVES, P], F32, name="sorted_words")
+                if step + 1 == FIRST_SORTED:
+                    sorted_words[step + 1] = sort_block(rows_sb[step + 1], nc.vector.tensor_copy)
                 for q in range(UNITS):
-                    is_sorted = step >= FIRST_SORTED and q < SCALAR_SORTS + VECTOR_SORTS
+                    is_sorted = step >= FIRST_SORTED and q < SORTED_UNITS
                     turn_unit(rows_sb[step], sorted_words[step] if is_sorted else None, grouped[step], q, nc.scalar.copy)
-                if sort_next:
-                    for q in range(SCALAR_SORTS + VECTOR_SORTS):
-                        sort_unit(rows_sb[step + 1], sorted_words[step + 1], q, nc.scalar.copy if q < SCALAR_SORTS else nc.vector.tensor_copy)
+                if FIRST_SORTED < step + SORT_AHEAD < n_blocks:
+                    sorted_words[step + SORT_AHEAD] = sort_block(rows_sb[step + SORT_AHEAD], nc.scalar.copy)
             if 0 <= w < n_weight_blocks - 1:
                 banks[w] = multiply_block([mx[t] for t in range(TOKEN_BLOCKS)], mx[w + TOKEN_BLOCKS])
             elif w == n_weight_blocks - 1:

from contextlib import ExitStack

import concourse.mybir as mybir
from concourse.masks import make_identity

F32 = mybir.dt.float32
BF16 = mybir.dt.bfloat16
U32 = mybir.dt.uint32
U8 = mybir.dt.uint8
FP8X4 = mybir.dt.float8_e4m3fn_x4
MULT = mybir.AluOpType.mult
ADD = mybir.AluOpType.add

P = 128
S = 512
K = 2048
D = 128
K_PASS = 4 * P
PASSES = K // K_PASS
WORDS_PASS = K_PASS // 2
HALVES = 2
ROW_TILES = 2
BLOCK = ROW_TILES * P
PAIR = 2
UNITS = ROW_TILES * PASSES // PAIR
TOKEN_BLOCKS = S // BLOCK
TOKEN_TILES = S // P
HEADS_BLOCK = BLOCK // D
STORE_COLS = 2 * BLOCK
PAIRED_STORES = 2048 // BLOCK
SPLIT_LOADS = 5
FIRST_SORTED = 5
SORTED_UNITS = 3
SORT_AHEAD = 2

FLOPS = 2 * S * K * (2048 + 512 + 512)


def tile_attention_pa_kernel(
    tc, x, wq_w, wk_w, wv_w, freqs_cos, freqs_sin, out_0, out_1, out_2
):
    nc = tc.nc
    with ExitStack() as ctx:
        ctx.enter_context(tc.manual_schedule())

        const = ctx.enter_context(tc.tile_pool(name="const", bufs=1))
        psum_turn = ctx.enter_context(tc.psum_pool(name="psum_turn", bufs=UNITS))
        psum_acc = ctx.enter_context(tc.psum_pool(name="psum_acc", bufs=2 * TOKEN_BLOCKS))

        row_blocks = [x[0].rearrange("(p b a) k -> b a p k", b=TOKEN_BLOCKS, a=ROW_TILES)[b] for b in range(TOKEN_BLOCKS)]
        weight_blocks = []
        for weight, out, rotated in ((wq_w, out_0, True), (wk_w, out_1, True), (wv_w, out_2, False)):
            out_view = out[0].rearrange("(p m) h d -> p m (h d)", m=TOKEN_TILES)
            blocks_view = weight.rearrange("(b p a) k -> b a p k", p=P, a=ROW_TILES)
            for b in range(weight.shape[0] // BLOCK):
                row_blocks.append(blocks_view[b])
                weight_blocks.append((out_view, b * BLOCK, rotated))
        n_blocks = len(row_blocks)
        n_weight_blocks = len(weight_blocks)

        rows_pool = ctx.enter_context(tc.tile_pool(name="rows", bufs=n_blocks))
        sorted_pool = ctx.enter_context(tc.tile_pool(name="sorted", bufs=SORT_AHEAD + 1))
        grouped_pool = ctx.enter_context(tc.tile_pool(name="grouped", bufs=3))
        x_mx_pool = ctx.enter_context(tc.tile_pool(name="x_mx", bufs=TOKEN_BLOCKS))
        w_mx_pool = ctx.enter_context(tc.tile_pool(name="w_mx", bufs=4))
        product_pool = ctx.enter_context(tc.tile_pool(name="product", bufs=4))
        result_pool = ctx.enter_context(tc.tile_pool(name="result", bufs=6))
        last_pool = ctx.enter_context(tc.tile_pool(name="last", bufs=TOKEN_TILES))

        cos_sb = const.tile([P, TOKEN_TILES, D // 2], BF16)
        sin_sb = const.tile([P, TOKEN_TILES, D // 2], BF16)
        rows_sb = []
        for block_rows in row_blocks:
            rows = rows_pool.tile([P, ROW_TILES, K], BF16)
            if len(rows_sb) < SPLIT_LOADS:
                for a in range(ROW_TILES):
                    nc.sync.dma_start(out=rows[:, a, :], in_=block_rows[a])
            else:
                nc.sync.dma_start(out=rows[:], in_=block_rows.rearrange("a p k -> p a k"))
            rows_sb.append(rows)
            if len(rows_sb) == TOKEN_BLOCKS + 2:
                nc.sync.dma_start(out=cos_sb[:], in_=freqs_cos.rearrange("(p m) j -> p m j", m=TOKEN_TILES))
                nc.sync.dma_start(out=sin_sb[:], in_=freqs_sin.rearrange("(p m) j -> p m j", m=TOKEN_TILES))

        ident = const.tile([P, P], F32)
        make_identity(nc, ident[:])
        factors = const.tile([P, TOKEN_TILES, 2, D // 2, 2], F32)
        nc.gpsimd.tensor_copy(out=factors[:, :, 0, :, 0:1], in_=cos_sb[:].unsqueeze(3))
        nc.gpsimd.tensor_copy(out=factors[:, :, 0, :, 1:2], in_=sin_sb[:].unsqueeze(3))
        nc.gpsimd.tensor_scalar_mul(out=factors[:, :, 1, :, 0:1], in0=sin_sb[:].unsqueeze(3), scalar1=-1.0)
        nc.gpsimd.tensor_copy(out=factors[:, :, 1, :, 1:2], in_=cos_sb[:].unsqueeze(3))

        def sort_block(rows, copy):
            sorted_words = sorted_pool.tile([P, SORTED_UNITS, PAIR, HALVES, P], F32, name="sorted_words")
            words = rows[:].rearrange("p a k -> p (a k)").bitcast(F32)
            copy(
                out=sorted_words[:].rearrange("p q g u j -> p (q g) u j"),
                in_=words[:, : SORTED_UNITS * PAIR * WORDS_PASS].rearrange("p (n j u) -> p n u j", n=SORTED_UNITS * PAIR, u=HALVES),
            )
            return sorted_words

        def turn_unit(rows, sorted_words, grouped, q, copy):
            a, pair = divmod(q, PASSES // PAIR)
            words = rows[:, a, :].bitcast(F32)
            bank = psum_turn.tile([P, PAIR, HALVES, P], F32, name="bank")
            for g in range(PAIR):
                for u in range(HALVES):
                    if sorted_words is None:
                        first = (pair * PAIR + g) * WORDS_PASS
                        half = words[:, first + u : first + WORDS_PASS : HALVES]
                    else:
                        half = sorted_words[:, q, g, u, :]
                    nc.tensor.transpose(bank[:, g, u, :], half, ident[:])
            copy(
                out=grouped[:]
                .bitcast(F32)
                .rearrange("p (g a r u) -> p g a r u", g=PASSES, a=ROW_TILES, u=HALVES)[:, pair * PAIR : (pair + 1) * PAIR, a],
                in_=bank[:].rearrange("p g u r -> p g r u"),
            )

        def quantise_block(pool, grouped):
            codes = pool.tile([P, PASSES * BLOCK], U32, align_bytes=64)
            scales = pool.tile([P, PASSES * BLOCK], U8, align_bytes=64)
            nc.vector.quantize_mx(out=codes[:].bitcast(FP8X4), scales=scales[:], in_=grouped[:])
            return codes, scales

        def multiply_tile(acc, x_mx, a, w_mx):
            x_codes, x_scales = x_mx
            w_codes, w_scales = w_mx
            for g in range(PASSES):
                tokens = slice(g * BLOCK + a * P, g * BLOCK + (a + 1) * P)
                features = slice(g * BLOCK, (g + 1) * BLOCK)
                nc.tensor.matmul_mx(
                    out=acc,
                    lhsT=x_codes[:, tokens].bitcast(FP8X4),
                    lhsT_scale=x_scales[:, tokens],
                    rhs=w_codes[:, features].bitcast(FP8X4),
                    rhs_scale=w_scales[:, features],
                    start=(g == 0),
                    stop=(g == PASSES - 1),
                )

        def multiply_block(x_mx, w_mx):
            banks = []
            for t in range(TOKEN_BLOCKS):
                acc = psum_acc.tile([P, ROW_TILES * BLOCK], F32, name="acc")
                for a in range(ROW_TILES):
                    multiply_tile(acc[:, a * BLOCK : (a + 1) * BLOCK], x_mx[t], a, w_mx)
                banks.append(acc)
            return banks

        def multiply_by_factors(product, acc, token_block, first, count):
            shape = [P, count, 2, HEADS_BLOCK, D // 2, 2]
            tiles = slice(token_block * ROW_TILES + first, token_block * ROW_TILES + first + count)
            nc.vector.tensor_tensor(
                out=product[:, first : first + count].rearrange("p m w (h j e) -> p m w h j e", h=HEADS_BLOCK, e=2),
                in0=acc[:, first * BLOCK : (first + count) * BLOCK]
                .rearrange("p (m w h j) -> p m w h j", m=count, w=2, h=HEADS_BLOCK)
                .unsqueeze(5)
                .to_broadcast(shape),
                in1=factors[:, tiles].unsqueeze(3).to_broadcast(shape),
                op=MULT,
            )

        results = {}
        late_adds = []
        held_stores = []

        def finish_block(w, banks):
            out_view, first_col, rotated = weight_blocks[w]
            store_cols = STORE_COLS if w < PAIRED_STORES else BLOCK
            store_first = first_col // store_cols * store_cols
            cols = slice(first_col - store_first, first_col - store_first + BLOCK)
            if first_col == store_first:
                for t in range(TOKEN_BLOCKS):
                    results[t] = result_pool.tile([P, ROW_TILES, store_cols], F32, name="result")
            if rotated:
                late_adds.clear()
                for t in range(TOKEN_BLOCKS):
                    product = product_pool.tile([P, ROW_TILES, 2, BLOCK], F32, name="product")
                    if t == 0:
                        for a in range(ROW_TILES):
                            multiply_by_factors(product, banks[t], t, a, 1)
                            nc.gpsimd.tensor_tensor(
                                out=results[t][:, a, cols], in0=product[:, a, 0, :], in1=product[:, a, 1, :], op=ADD
                            )
                    else:
                        multiply_by_factors(product, banks[t], t, 0, ROW_TILES)
                        late_adds.append((results[t][:, :, cols], product[:, :, 0, :], product[:, :, 1, :]))
            else:
                for t in range(TOKEN_BLOCKS):
                    nc.scalar.copy(
                        out=results[t][:, :, cols].rearrange("p m (r e) -> p m r e", e=2),
                        in_=banks[t][:].rearrange("p (m e r) -> p m r e", m=ROW_TILES, e=2),
                    )

        def store_block(w):
            out_view, first_col, rotated = weight_blocks[w]
            store_cols = STORE_COLS if w < PAIRED_STORES else BLOCK
            store_first = first_col // store_cols * store_cols
            for out, in0, in1 in late_adds:
                nc.vector.tensor_tensor(out=out, in0=in0, in1=in1, op=ADD)
            late_adds.clear()
            if first_col + BLOCK == store_first + store_cols:
                stores = [
                    (out_view[:, t * ROW_TILES : (t + 1) * ROW_TILES, store_first : store_first + store_cols], results[t])
                    for t in range(TOKEN_BLOCKS)
                ]
                if rotated and not weight_blocks[w + 1][2]:
                    held_stores.extend(stores)
                    return
                for out, result in stores + held_stores:
                    nc.sync.dma_start(out=out, in_=result[:])
                held_stores.clear()

        def multiply_and_finish_last_block(x_mx, w_mx):
            out_view, first_col, rotated = weight_blocks[n_weight_blocks - 1]
            assert not rotated
            for m in range(TOKEN_TILES):
                t, a = divmod(m, ROW_TILES)
                acc = psum_turn.tile([P, BLOCK], F32, name="bank")
                multiply_tile(acc[:], x_mx[t], a, w_mx)
                last = last_pool.tile([P, BLOCK], F32)
                nc.scalar.copy(out=last[:].rearrange("p (r e) -> p r e", e=2), in_=acc[:].rearrange("p (e r) -> p r e", e=2))
                nc.sync.dma_start(out=out_view[:, m, first_col : first_col + BLOCK], in_=last[:])

        sorted_words = {}
        grouped = {}
        mx = {}
        banks = {}
        for step in range(n_blocks + 2):
            w = step - 2 - TOKEN_BLOCKS
            quantise_first = step - 1 == n_blocks - 1
            if quantise_first:
                mx[step - 1] = quantise_block(w_mx_pool, grouped[step - 1])
            if 0 <= w - 1 < n_weight_blocks - 1:
                finish_block(w - 1, banks[w - 1])
            if 0 <= step - 1 < n_blocks and not quantise_first:
                pool = x_mx_pool if step - 1 < TOKEN_BLOCKS else w_mx_pool
                mx[step - 1] = quantise_block(pool, grouped[step - 1])
            if 0 <= w - 1 < n_weight_blocks - 1:
                store_block(w - 1)
            if step < n_blocks:
                grouped[step] = grouped_pool.tile([P, PASSES * BLOCK * 4], BF16, align_bytes=64, name="grouped")
                if step + 1 == FIRST_SORTED:
                    sorted_words[step + 1] = sort_block(rows_sb[step + 1], nc.vector.tensor_copy)
                for q in range(UNITS):
                    is_sorted = step >= FIRST_SORTED and q < SORTED_UNITS
                    turn_unit(rows_sb[step], sorted_words[step] if is_sorted else None, grouped[step], q, nc.scalar.copy)
                if FIRST_SORTED < step + SORT_AHEAD < n_blocks:
                    sorted_words[step + SORT_AHEAD] = sort_block(rows_sb[step + SORT_AHEAD], nc.scalar.copy)
            if 0 <= w < n_weight_blocks - 1:
                banks[w] = multiply_block([mx[t] for t in range(TOKEN_BLOCKS)], mx[w + TOKEN_BLOCKS])
            elif w == n_weight_blocks - 1:
                multiply_and_finish_last_block([mx[t] for t in range(TOKEN_BLOCKS)], mx[w + TOKEN_BLOCKS])
